import numpy as np
import ml_dtypes


def mxq(x, axis, fmt="e4m3"):
    dtype, down = {"e4m3": (ml_dtypes.float8_e4m3fn, 7), "e5m2": (ml_dtypes.float8_e5m2, 14)}[fmt]
    v = np.moveaxis(np.asarray(x, np.float32).astype(ml_dtypes.bfloat16).astype(np.float64), axis, -1)
    blocks = v.reshape(v.shape[:-1] + (-1, 32))
    amax = np.abs(blocks).max(-1, keepdims=True)
    byte = np.maximum(np.where(amax > 0, np.frexp(amax)[1] - 1 + 127, 0) - down, 1)
    scale = np.exp2(byte - 127.0)
    codes = (blocks / scale).astype(np.float32).astype(dtype).astype(np.float64)
    return np.moveaxis((codes * scale).reshape(v.shape), -1, axis)


WIDE = False


def mx_kscale(k):
    if not WIDE:
        return np.ones(k)
    levels = np.array([10, -10, 5, -5, 0])
    a = np.random.permutation(np.resize(levels, k // 512 * 4)).reshape(k // 512, 4)
    idx = np.arange(k)
    return np.exp2(a[idx // 512, idx % 128 // 32])


BF16 = ml_dtypes.bfloat16


def bf(x):
    return np.asarray(x, np.float32).astype(BF16)


def f64(x):
    return np.asarray(x).astype(np.float64)


E2M1 = np.array([0.0, 0.5, 1.0, 1.5, 2.0, 3.0, 4.0, 6.0, -0.0, -0.5, -1.0, -1.5, -2.0, -3.0, -4.0, -6.0])


def pack_weight(w, fmt):
    k, n = w.shape
    w = f64(bf(w)).reshape(k // 32, 32, n)
    amax = np.abs(w).max(1)
    if fmt == "e4m3":
        byte = np.frexp(amax)[1] - 1 + 127 - 7
    else:
        mant, ex = np.frexp(amax / 6.0)
        byte = np.where(mant > 0.5, ex, ex - 1) + 127
    byte = np.clip(np.where(amax > 0, byte, 1), 1, 254)
    scaled = (w * np.exp2(127.0 - byte)[:, None, :]).reshape(k, n).astype(np.float32)
    by_word = np.ascontiguousarray(scaled.reshape(k // 512, 128, 4, n).transpose(0, 1, 3, 2))
    if fmt == "e4m3":
        words = by_word.astype(ml_dtypes.float8_e4m3fn).view(np.uint8)
    else:
        c = by_word.astype(ml_dtypes.float4_e2m1fn).view(np.uint8) & 0xF
        words = c[..., 0::2] | (c[..., 1::2] << 4)
    return np.ascontiguousarray(words), np.ascontiguousarray(byte.astype(np.uint8).reshape(k // 512, 16, n))


def unpack_weight(words, scales, fmt):
    g, p, n, _ = words.shape
    if fmt == "e4m3":
        vals = np.ascontiguousarray(words).view(ml_dtypes.float8_e4m3fn).astype(np.float64)
    else:
        nib = np.empty((g, p, n, 4), np.uint8)
        nib[..., 0::2] = words & 0xF
        nib[..., 1::2] = words >> 4
        vals = E2M1[nib]
    vals = vals * np.repeat(np.exp2(scales.astype(np.float64) - 127.0), 8, axis=1)[..., None]
    return vals.transpose(0, 1, 3, 2).reshape(g * 512, n)


B, N, M, H, O = 64, 2, 2, 16384, 512


def rotary(x):
    S, F = x.shape[1], x.shape[2]
    pos = np.arange(S, dtype=np.float64)[:, None]
    inv_freq = np.power(10000.0, -2.0 * np.arange(F // 2, dtype=np.float64) / F)
    ang = pos * inv_freq
    cos = np.repeat(np.cos(ang), 2, axis=-1)
    sin = np.repeat(np.sin(ang), 2, axis=-1)
    x_rot = np.stack([-x[..., 1::2], x[..., ::2]], axis=-1).reshape(x.shape)
    return x * cos + x_rot * sin


def setup_inputs():
    s = np.repeat(mx_kscale(H)[::2], 2)
    t = np.repeat(mx_kscale(H)[::2], 2)
    review = bf(np.random.standard_normal((B, N, H)) * s)
    reply = bf(np.random.standard_normal((B, M, H)) * t)
    w = np.random.standard_normal((O, 2 * H)) * 0.7 / np.sqrt(H) / np.concatenate([s, t])
    words, scales = pack_weight(w.T, "e4m3")
    b = bf(np.random.standard_normal(O) * 0.5)
    return {"review": review,
            "reply": reply,
            "W_words": words,
            "W_scales": scales,
            "b": b}


def reference(review, reply, W_words, W_scales, b):
    review = rotary(f64(review))
    reply = rotary(f64(reply))
    W = unpack_weight(W_words, W_scales, "e4m3")
    W_r, W_p = W[:H], W[H:]
    proj_review = mxq(review, 2, "e4m3") @ W_r
    proj_reply = mxq(reply, 2, "e4m3") @ W_p
    out = proj_review[:, :, None, :] + proj_reply[:, None, :, :] + f64(b)
    return np.maximum(out, 0.0)

@@ -1,0 +1,282 @@
+import math
+from contextlib import ExitStack
+
+import concourse.mybir as mybir
+from concourse.masks import make_identity
+
+F32 = mybir.dt.float32
+BF16 = mybir.dt.bfloat16
+I32 = mybir.dt.int32
+U32 = mybir.dt.uint32
+U8 = mybir.dt.uint8
+FP8X4 = mybir.dt.float8_e4m3fn_x4
+ALU = mybir.AluOpType
+ACT = mybir.ActivationFunctionType
+
+P = 128
+BATCH = 64
+FEATURES = 16384
+OUT_COLS = 512
+K_PASS = 512
+PASSES = FEATURES // K_PASS
+WORDS_PASS = K_PASS // 2
+
+REPLY, REVIEW = 0, 1
+W_FIRST_GROUP = (PASSES, 0)
+
+ROUND_G = 2
+ROUNDS = PASSES // ROUND_G
+X_CHUNK_G = 8
+X_CHUNKS = PASSES // X_CHUNK_G
+W_CHUNK_G = 4
+W_BUFS = 8
+PLANE_GROUPS = 16
+MX_LAG = 6
+
+FLOPS = 2 * 2 * P * FEATURES * OUT_COLS
+
+
+def tile_positionwisedtableencoder_k_kernel(tc, review, reply, W_words, W_scales, b, out):
+    nc = tc.nc
+    rows = {
+        REPLY: reply.rearrange("j n h -> (j n) h"),
+        REVIEW: review.rearrange("j n h -> (j n) h"),
+    }
+    scale_words = W_scales.bitcast(F32)
+
+    w_chunks = []
+    for c in range(X_CHUNKS):
+        for o in (REPLY, REVIEW):
+            for first in range(c * X_CHUNK_G, (c + 1) * X_CHUNK_G, W_CHUNK_G):
+                w_chunks.append((o, first))
+
+    with ExitStack() as ctx:
+        ctx.enter_context(tc.manual_schedule())
+        const = ctx.enter_context(tc.tile_pool(name="const", bufs=1))
+        x_pool = ctx.enter_context(tc.tile_pool(name="x", bufs=1))
+        w_pool = ctx.enter_context(tc.tile_pool(name="w", bufs=W_BUFS))
+        code_pool = ctx.enter_context(tc.tile_pool(name="codes", bufs=1))
+        cos_pool = ctx.enter_context(tc.tile_pool(name="cospart", bufs=4))
+        plane_pool = ctx.enter_context(tc.tile_pool(name="turned", bufs=2))
+        group_pool = ctx.enter_context(tc.tile_pool(name="grouped", bufs=3))
+        bank_pool = ctx.enter_context(tc.psum_pool(name="banks", bufs=4))
+        acc_pool = ctx.enter_context(tc.psum_pool(name="acc", bufs=1))
+        spread_pool = ctx.enter_context(tc.psum_pool(name="spread", bufs=2))
+
+        x_sb = {}
+        for c in range(X_CHUNKS):
+            for o in (REPLY, REVIEW):
+                x_tile = x_pool.tile([P, X_CHUNK_G * K_PASS], BF16, name="x%d_%d" % (o, c))
+                cols = slice(c * X_CHUNK_G * K_PASS, (c + 1) * X_CHUNK_G * K_PASS)
+                nc.sync.dma_start(out=x_tile[:], in_=rows[o][:, cols])
+                x_sb[o, c] = x_tile
+
+        w_sb = {}
+
+        def load_weights(w):
+            o, first = w_chunks[w]
+            group = W_FIRST_GROUP[o] + first
+            w_tile = w_pool.tile([P, W_CHUNK_G, OUT_COLS], I32, name="w_tile", align_bytes=64)
+            nc.sync.dma_start(
+                out=w_tile[:],
+                in_=W_words[group : group + W_CHUNK_G].rearrange("g p n t -> p g (n t)").bitcast(I32),
+            )
+            w_sb[w] = w_tile
+
+        for w in range(W_BUFS):
+            load_weights(w)
+
+        w_planes = const.tile([P, PLANE_GROUPS, OUT_COLS], U8, name="w_planes", align_bytes=64)
+        nc.vector.memset(w_planes[:].rearrange("p a n -> p (a n)").bitcast(I32), 0)
+
+        bias_row = const.tile([P, OUT_COLS], BF16, name="bias_row")
+        ones = const.tile([P, P], BF16, name="ones")
+        bias_sb = const.tile([P, OUT_COLS], F32, name="bias_sb")
+        nc.vector.memset(bias_row[:], 0.0)
+        nc.scalar.dma_start(out=bias_row[0:1, :], in_=b.unsqueeze(0))
+        nc.vector.memset(ones[:], 1.0)
+
+        def spread_bias():
+            bias_ps = spread_pool.tile([P, OUT_COLS], F32, name="bias_ps", tag="spread")
+            nc.tensor.matmul(out=bias_ps[:], lhsT=ones[:], rhs=bias_row[:], start=True, stop=True)
+            nc.scalar.copy(out=bias_sb[:], in_=bias_ps[:])
+
+        ident = const.tile([P, P], F32, name="ident")
+        make_identity(nc, ident[:])
+        pair_index = const.tile([P, 2 * PASSES], I32, name="pair_index")
+        nc.gpsimd.iota(pair_index[:], pattern=[[WORDS_PASS, PASSES], [1, 2]], base=0, channel_multiplier=2)
+
+        for half in range(2):
+            for o in (REPLY, REVIEW):
+                group = W_FIRST_GROUP[o] + half * PLANE_GROUPS
+                plane_row = 4 * (group // PLANE_GROUPS)
+                for r in range(4):
+                    nc.gpsimd.dma_start(
+                        out=w_planes[plane_row + r : P : 32, :, :].bitcast(F32),
+                        in_=scale_words[group : group + PLANE_GROUPS, r : 16 : 4, :].rearrange("g q n -> q g n"),
+                    )
+
+        pair_f = const.tile([P, 2 * PASSES], F32, name="pair_f")
+        angle = const.tile([P, 2 * PASSES], F32, name="angle")
+        sin_tab = const.tile([P, 2 * PASSES], F32, name="sin_tab")
+        neg_sin = const.tile([P, 2 * PASSES], F32, name="neg_sin")
+        half_sin = const.tile([P, 2 * PASSES], F32, name="half_sin")
+        half_sq = const.tile([P, 2 * PASSES], F32, name="half_sq")
+        cos_tab = const.tile([P, 2 * PASSES], F32, name="cos_tab")
+        nc.vector.tensor_copy(out=pair_f[:], in_=pair_index[:])
+        nc.scalar.activation(out=angle[:], in_=pair_f[:], func=ACT.Exp, scale=-2.0 * math.log(10000.0) / FEATURES)
+        nc.scalar.activation(out=sin_tab[:], in_=angle[:], func=ACT.Sin)
+        nc.scalar.activation(out=half_sin[:], in_=angle[:], func=ACT.Sin, scale=0.5)
+        nc.scalar.activation(out=half_sq[:], in_=half_sin[:], func=ACT.Square)
+
+        perm = const.tile([P, P], F32, name="perm")
+        nc.vector.tensor_copy(
+            out=perm[:].rearrange("p (n j) -> p n j", n=2),
+            in_=ident[:].rearrange("p (j n) -> p n j", n=2),
+        )
+        select = const.tile([P, 2, 2, BATCH], F32, name="select")
+        nc.vector.tensor_copy(
+            out=select[:],
+            in_=ident[:].rearrange("p (m j) -> p m j", m=2).unsqueeze(2).to_broadcast([P, 2, 2, BATCH]),
+        )
+        nc.vector.tensor_scalar(
+            out=cos_tab[:], in0=half_sq[:], scalar1=-2.0, scalar2=1.0, op0=ALU.mult, op1=ALU.add
+        )
+        nc.vector.tensor_scalar_mul(out=neg_sin[:], in0=sin_tab[:], scalar1=-1.0)
+
+        acc = {
+            REPLY: acc_pool.tile([P, OUT_COLS], F32, name="acc_reply"),
+            REVIEW: acc_pool.tile([P, OUT_COLS], F32, name="acc_review"),
+        }
+        banks = {}
+        grouped = {}
+        turned = {}
+        codes = {}
+        x_planes = {}
+
+        def transpose_round(k):
+            for g in range(k * ROUND_G, (k + 1) * ROUND_G):
+                c, g_in_chunk = divmod(g, X_CHUNK_G)
+                bank = bank_pool.tile([P, 2, 2, P], F32, name="bank")
+                for o in (REPLY, REVIEW):
+                    words = x_sb[o, c][:].bitcast(F32)
+                    for u in range(2):
+                        nc.tensor.transpose(
+                            out=bank[:, o, u, :],
+                            in_=words[:, g_in_chunk * WORDS_PASS + u : (g_in_chunk + 1) * WORDS_PASS : 2],
+                            identity=perm[:],
+                        )
+                banks[g] = bank
+
+        def rotate_round(k):
+            grouped[k] = group_pool.tile([P, ROUND_G, 2, P, 4], BF16, name="grouped", align_bytes=64)
+            turned[k] = plane_pool.tile([P, ROUND_G, 2, 4, BATCH], BF16, name="turned")
+            for g_in_round in range(ROUND_G):
+                g = k * ROUND_G + g_in_round
+                bank = banks[g]
+                nc.scalar.copy(
+                    out=grouped[k][:, g_in_round, :, 0:BATCH, :].bitcast(F32),
+                    in_=bank[:, :, :, 0:BATCH].rearrange("p o u j -> p o j u"),
+                )
+                position1 = bank[:].bitcast(BF16)[:, :, :, P : 2 * P]
+                cos_part = cos_pool.tile([P, 2, 2, P], F32, name="cos_part")
+                for u in range(2):
+                    col = 2 * g + u
+                    nc.scalar.activation(
+                        out=cos_part[:, u, :, :],
+                        in_=position1[:, :, u, :],
+                        func=ACT.Copy,
+                        scale=cos_tab[:, col : col + 1],
+                    )
+                x_pairs = position1.rearrange("p o u (j e) -> p o u j e", e=2)
+                cos_pairs = cos_part[:].rearrange("p u o (j e) -> p u o j e", e=2)
+                for u in range(2):
+                    col = 2 * g + u
+                    nc.vector.scalar_tensor_tensor(
+                        out=turned[k][:, g_in_round, :, 2 * u, :],
+                        in0=x_pairs[:, :, u, :, 1],
+                        scalar=neg_sin[:, col : col + 1],
+                        in1=cos_pairs[:, u, :, :, 0],
+                        op0=ALU.mult,
+                        op1=ALU.add,
+                    )
+                    nc.vector.scalar_tensor_tensor(
+                        out=turned[k][:, g_in_round, :, 2 * u + 1, :],
+                        in0=x_pairs[:, :, u, :, 0],
+                        scalar=sin_tab[:, col : col + 1],
+                        in1=cos_pairs[:, u, :, :, 1],
+                        op0=ALU.mult,
+                        op1=ALU.add,
+                    )
+
+        def regroup_round(k):
+            nc.vector.tensor_copy(
+                out=grouped[k][:, :, :, BATCH:P, :],
+                in_=turned[k][:].rearrange("p g o t j -> p g o j t"),
+            )
+
+        def quantise_round(k):
+            codes[k] = code_pool.tile([P, ROUND_G, 2, P], U32, name="codes%d" % k, align_bytes=64)
+            x_planes[k] = code_pool.tile([P, ROUND_G, 2, P], U8, name="x_planes%d" % k, align_bytes=64)
+            nc.vector.quantize_mx(
+                out=codes[k][:].rearrange("p g o c -> p (g o c)").bitcast(FP8X4),
+                scales=x_planes[k][:].rearrange("p g o c -> p (g o c)"),
+                in_=grouped[k][:].rearrange("p g o c t -> p (g o c t)"),
+            )
+
+        def multiply_chunk(w):
+            o, first = w_chunks[w]
+            for g in range(first, first + W_CHUNK_G):
+                k, g_in_round = divmod(g, ROUND_G)
+                plane, block = divmod(W_FIRST_GROUP[o] + g, PLANE_GROUPS)
+                nc.tensor.matmul_mx(
+                    out=acc[o][:],
+                    lhsT=codes[k][:, g_in_round, o, :].bitcast(FP8X4),
+                    lhsT_scale=x_planes[k][:, g_in_round, o, :],
+                    rhs=w_sb[w][:, g - first, :].bitcast(FP8X4),
+                    rhs_scale=w_planes[4 * plane : P, block, :],
+                    start=(g == 0),
+                    stop=(g == PASSES - 1),
+                )
+
+        reply_sb = const.tile([P, OUT_COLS], F32, name="reply_sb")
+        addend = const.tile([P, 2, OUT_COLS], F32, name="addend")
+
+        def spread_reply():
+            nc.vector.tensor_tensor(out=reply_sb[:], in0=acc[REPLY][:], in1=bias_sb[:], op=ALU.add)
+            for m in range(2):
+                spread = spread_pool.tile([P, OUT_COLS], F32, name="spread", tag="spread")
+                nc.tensor.matmul(
+                    out=spread[:],
+                    lhsT=select[:, m, :, :].rearrange("p n j -> p (n j)"),
+                    rhs=reply_sb[:],
+                    start=True,
+                    stop=True,
+                )
+                nc.scalar.copy(out=addend[:, m, :], in_=spread[:])
+
+        for step in range(ROUNDS + MX_LAG):
+            if step < ROUNDS:
+                transpose_round(step)
+                rotate_round(step)
+            if 1 <= step <= ROUNDS:
+                quantise_round(step - 1)
+            if step < ROUNDS:
+                regroup_round(step)
+            w = step - MX_LAG
+            if w == 0:
+                spread_bias()
+            if w >= 0:
+                multiply_chunk(w)
+                if w + W_BUFS < len(w_chunks):
+                    load_weights(w + W_BUFS)
+                if w_chunks[w] == (REPLY, PASSES - W_CHUNK_G):
+                    spread_reply()
+
+        summed = const.tile([P, 2, OUT_COLS], F32, name="summed")
+        result = const.tile([P, 2, OUT_COLS], F32, name="result")
+        for m in range(2):
+            nc.vector.tensor_tensor(out=summed[:, m, :], in0=acc[REVIEW][:], in1=addend[:, m, :], op=ALU.add)
+            nc.scalar.activation(out=result[:, m, :], in_=summed[:, m, :], func=ACT.Relu)
+            for n in range(2):
+                nc.sync.dma_start(out=out[:, n, m, :], in_=result[n * BATCH : (n + 1) * BATCH, m, :])

@@ -42,7 +42,7 @@ def tile_positionwisedtableencoder_k_kernel(tc, review, reply, W_words, W_scales
         REPLY: reply.rearrange("j n h -> (j n) h"),
         REVIEW: review.rearrange("j n h -> (j n) h"),
     }
-    scale_words = W_scales.bitcast(F32)
+    scale_words = W_scales.bitcast(I32)
 
     w_chunks = []
     for c in range(X_CHUNKS):
@@ -71,6 +71,15 @@ def tile_positionwisedtableencoder_k_kernel(tc, review, reply, W_words, W_scales
                 nc.sync.dma_start(out=x_tile[:], in_=rows[o][:, cols])
                 x_sb[o, c] = x_tile
 
+        w_planes = const.tile([P, PLANE_GROUPS, OUT_COLS], U8, name="w_planes", align_bytes=64)
+        nc.vector.memset(w_planes[:].rearrange("p a n -> p (a n)").bitcast(I32), 0)
+        for q in range(16):
+            first_row = 32 * (q // 4) + q % 4
+            nc.sync.dma_start(
+                out=w_planes[first_row : first_row + 16 : 4, :, :].bitcast(I32),
+                in_=scale_words[:, q, :].rearrange("(s a) n -> s a n", a=PLANE_GROUPS),
+            )
+
         w_sb = {}
 
         def load_weights(w):
@@ -85,9 +94,6 @@ def tile_positionwisedtableencoder_k_kernel(tc, review, reply, W_words, W_scales
 
         for w in range(W_BUFS):
             load_weights(w)
-
-        w_planes = const.tile([P, PLANE_GROUPS, OUT_COLS], U8, name="w_planes", align_bytes=64)
-        nc.vector.memset(w_planes[:].rearrange("p a n -> p (a n)").bitcast(I32), 0)
 
         bias_row = const.tile([P, OUT_COLS], BF16, name="bias_row")
         ones = const.tile([P, P], BF16, name="ones")
@@ -105,16 +111,6 @@ def tile_positionwisedtableencoder_k_kernel(tc, review, reply, W_words, W_scales
         make_identity(nc, ident[:])
         pair_index = const.tile([P, 2 * PASSES], I32, name="pair_index")
         nc.gpsimd.iota(pair_index[:], pattern=[[WORDS_PASS, PASSES], [1, 2]], base=0, channel_multiplier=2)
-
-        for half in range(2):
-            for o in (REPLY, REVIEW):
-                group = W_FIRST_GROUP[o] + half * PLANE_GROUPS
-                plane_row = 4 * (group // PLANE_GROUPS)
-                for r in range(4):
-                    nc.gpsimd.dma_start(
-                        out=w_planes[plane_row + r : P : 32, :, :].bitcast(F32),
-                        in_=scale_words[group : group + PLANE_GROUPS, r : 16 : 4, :].rearrange("g q n -> q g n"),
-                    )
 
         pair_f = const.tile([P, 2 * PASSES], F32, name="pair_f")
         angle = const.tile([P, 2 * PASSES], F32, name="angle")

@@ -42,7 +42,6 @@ def tile_positionwisedtableencoder_k_kernel(tc, review, reply, W_words, W_scales
         REPLY: reply.rearrange("j n h -> (j n) h"),
         REVIEW: review.rearrange("j n h -> (j n) h"),
     }
-    scale_words = W_scales.bitcast(I32)
 
     w_chunks = []
     for c in range(X_CHUNKS):
@@ -73,12 +72,20 @@ def tile_positionwisedtableencoder_k_kernel(tc, review, reply, W_words, W_scales
 
         w_planes = const.tile([P, PLANE_GROUPS, OUT_COLS], U8, name="w_planes", align_bytes=64)
         nc.vector.memset(w_planes[:].rearrange("p a n -> p (a n)").bitcast(I32), 0)
-        for q in range(16):
-            first_row = 32 * (q // 4) + q % 4
-            nc.sync.dma_start(
-                out=w_planes[first_row : first_row + 16 : 4, :, :].bitcast(I32),
-                in_=scale_words[:, q, :].rearrange("(s a) n -> s a n", a=PLANE_GROUPS),
-            )
+
+        def load_planes(queue, view, half):
+            for o in (REPLY, REVIEW):
+                group = W_FIRST_GROUP[o] + half * PLANE_GROUPS
+                plane_row = 4 * (group // PLANE_GROUPS)
+                for r in range(4):
+                    queue.dma_start(
+                        out=w_planes[plane_row + r : P : 32, :, :].bitcast(view),
+                        in_=W_scales.bitcast(view)[group : group + PLANE_GROUPS, r : 16 : 4, :].rearrange(
+                            "g q n -> q g n"
+                        ),
+                    )
+
+        load_planes(nc.sync, I32, 0)
 
         w_sb = {}
 
@@ -111,6 +118,7 @@ def tile_positionwisedtableencoder_k_kernel(tc, review, reply, W_words, W_scales
         make_identity(nc, ident[:])
         pair_index = const.tile([P, 2 * PASSES], I32, name="pair_index")
         nc.gpsimd.iota(pair_index[:], pattern=[[WORDS_PASS, PASSES], [1, 2]], base=0, channel_multiplier=2)
+        load_planes(nc.gpsimd, F32, 1)
 
         pair_f = const.tile([P, 2 * PASSES], F32, name="pair_f")
         angle = const.tile([P, 2 * PASSES], F32, name="angle")

@@ -42,6 +42,7 @@ def tile_positionwisedtableencoder_k_kernel(tc, review, reply, W_words, W_scales
         REPLY: reply.rearrange("j n h -> (j n) h"),
         REVIEW: review.rearrange("j n h -> (j n) h"),
     }
+    scale_words = W_scales.bitcast(I32)
 
     w_chunks = []
     for c in range(X_CHUNKS):
@@ -60,7 +61,7 @@ def tile_positionwisedtableencoder_k_kernel(tc, review, reply, W_words, W_scales
         group_pool = ctx.enter_context(tc.tile_pool(name="grouped", bufs=3))
         bank_pool = ctx.enter_context(tc.psum_pool(name="banks", bufs=4))
         acc_pool = ctx.enter_context(tc.psum_pool(name="acc", bufs=1))
-        spread_pool = ctx.enter_context(tc.psum_pool(name="spread", bufs=2))
+        spread_pool = ctx.enter_context(tc.psum_pool(name="spread", bufs=1))
 
         x_sb = {}
         for c in range(X_CHUNKS):
@@ -72,20 +73,12 @@ def tile_positionwisedtableencoder_k_kernel(tc, review, reply, W_words, W_scales
 
         w_planes = const.tile([P, PLANE_GROUPS, OUT_COLS], U8, name="w_planes", align_bytes=64)
         nc.vector.memset(w_planes[:].rearrange("p a n -> p (a n)").bitcast(I32), 0)
-
-        def load_planes(queue, view, half):
-            for o in (REPLY, REVIEW):
-                group = W_FIRST_GROUP[o] + half * PLANE_GROUPS
-                plane_row = 4 * (group // PLANE_GROUPS)
-                for r in range(4):
-                    queue.dma_start(
-                        out=w_planes[plane_row + r : P : 32, :, :].bitcast(view),
-                        in_=W_scales.bitcast(view)[group : group + PLANE_GROUPS, r : 16 : 4, :].rearrange(
-                            "g q n -> q g n"
-                        ),
-                    )
-
-        load_planes(nc.sync, I32, 0)
+        for q in range(16):
+            first_row = 32 * (q // 4) + q % 4
+            nc.sync.dma_start(
+                out=w_planes[first_row : first_row + 16 : 4, :, :].bitcast(I32),
+                in_=scale_words[:, q, :].rearrange("(s a) n -> s a n", a=PLANE_GROUPS),
+            )
 
         w_sb = {}
 
@@ -93,10 +86,12 @@ def tile_positionwisedtableencoder_k_kernel(tc, review, reply, W_words, W_scales
             o, first = w_chunks[w]
             group = W_FIRST_GROUP[o] + first
             w_tile = w_pool.tile([P, W_CHUNK_G, OUT_COLS], I32, name="w_tile", align_bytes=64)
-            nc.sync.dma_start(
-                out=w_tile[:],
-                in_=W_words[group : group + W_CHUNK_G].rearrange("g p n t -> p g (n t)").bitcast(I32),
-            )
+            piece = 1 if w == len(w_chunks) - 1 else W_CHUNK_G
+            for i in range(0, W_CHUNK_G, piece):
+                nc.sync.dma_start(
+                    out=w_tile[:, i : i + piece, :],
+                    in_=W_words[group + i : group + i + piece].rearrange("g p n t -> p g (n t)").bitcast(I32),
+                )
             w_sb[w] = w_tile
 
         for w in range(W_BUFS):
@@ -118,7 +113,6 @@ def tile_positionwisedtableencoder_k_kernel(tc, review, reply, W_words, W_scales
         make_identity(nc, ident[:])
         pair_index = const.tile([P, 2 * PASSES], I32, name="pair_index")
         nc.gpsimd.iota(pair_index[:], pattern=[[WORDS_PASS, PASSES], [1, 2]], base=0, channel_multiplier=2)
-        load_planes(nc.gpsimd, F32, 1)
 
         pair_f = const.tile([P, 2 * PASSES], F32, name="pair_f")
         angle = const.tile([P, 2 * PASSES], F32, name="angle")
@@ -138,11 +132,9 @@ def tile_positionwisedtableencoder_k_kernel(tc, review, reply, W_words, W_scales
             out=perm[:].rearrange("p (n j) -> p n j", n=2),
             in_=ident[:].rearrange("p (j n) -> p n j", n=2),
         )
-        select = const.tile([P, 2, 2, BATCH], F32, name="select")
-        nc.vector.tensor_copy(
-            out=select[:],
-            in_=ident[:].rearrange("p (m j) -> p m j", m=2).unsqueeze(2).to_broadcast([P, 2, 2, BATCH]),
-        )
+        swap = const.tile([P, P], F32, name="swap")
+        nc.vector.tensor_copy(out=swap[:, 0:BATCH], in_=ident[:, BATCH:P])
+        nc.vector.tensor_copy(out=swap[:, BATCH:P], in_=ident[:, 0:BATCH])
         nc.vector.tensor_scalar(
             out=cos_tab[:], in0=half_sq[:], scalar1=-2.0, scalar2=1.0, op0=ALU.mult, op1=ALU.add
         )
@@ -243,21 +235,13 @@ def tile_positionwisedtableencoder_k_kernel(tc, review, reply, W_words, W_scales
                     stop=(g == PASSES - 1),
                 )
 
-        reply_sb = const.tile([P, OUT_COLS], F32, name="reply_sb")
         addend = const.tile([P, 2, OUT_COLS], F32, name="addend")
 
         def spread_reply():
-            nc.vector.tensor_tensor(out=reply_sb[:], in0=acc[REPLY][:], in1=bias_sb[:], op=ALU.add)
-            for m in range(2):
-                spread = spread_pool.tile([P, OUT_COLS], F32, name="spread", tag="spread")
-                nc.tensor.matmul(
-                    out=spread[:],
-                    lhsT=select[:, m, :, :].rearrange("p n j -> p (n j)"),
-                    rhs=reply_sb[:],
-                    start=True,
-                    stop=True,
-                )
-                nc.scalar.copy(out=addend[:, m, :], in_=spread[:])
+            nc.vector.tensor_tensor(out=addend[:, 0, :], in0=acc[REPLY][:], in1=bias_sb[:], op=ALU.add)
+            swapped = spread_pool.tile([P, OUT_COLS], F32, name="swapped", tag="spread")
+            nc.tensor.matmul(out=swapped[:], lhsT=swap[:], rhs=addend[:, 0, :], start=True, stop=True)
+            nc.scalar.copy(out=addend[:, 1, :], in_=swapped[:])
 
         for step in range(ROUNDS + MX_LAG):
             if step < ROUNDS:
@@ -279,8 +263,10 @@ def tile_positionwisedtableencoder_k_kernel(tc, review, reply, W_words, W_scales
 
         summed = const.tile([P, 2, OUT_COLS], F32, name="summed")
         result = const.tile([P, 2, OUT_COLS], F32, name="result")
-        for m in range(2):
-            nc.vector.tensor_tensor(out=summed[:, m, :], in0=acc[REVIEW][:], in1=addend[:, m, :], op=ALU.add)
-            nc.scalar.activation(out=result[:, m, :], in_=summed[:, m, :], func=ACT.Relu)
+        for d in range(2):
+            nc.vector.tensor_tensor(out=summed[:, d, :], in0=acc[REVIEW][:], in1=addend[:, d, :], op=ALU.add)
+        for d in range(2):
+            nc.vector.tensor_scalar_max(out=result[:, d, :], in0=summed[:, d, :], scalar1=0.0)
             for n in range(2):
-                nc.sync.dma_start(out=out[:, n, m, :], in_=result[n * BATCH : (n + 1) * BATCH, m, :])
+                m = (n + d) % 2
+                nc.sync.dma_start(out=out[:, n, m, :], in_=result[n * BATCH : (n + 1) * BATCH, d, :])

@@ -86,7 +86,7 @@ def tile_positionwisedtableencoder_k_kernel(tc, review, reply, W_words, W_scales
             o, first = w_chunks[w]
             group = W_FIRST_GROUP[o] + first
             w_tile = w_pool.tile([P, W_CHUNK_G, OUT_COLS], I32, name="w_tile", align_bytes=64)
-            piece = 1 if w == len(w_chunks) - 1 else W_CHUNK_G
+            piece = 1
             for i in range(0, W_CHUNK_G, piece):
                 nc.sync.dma_start(
                     out=w_tile[:, i : i + piece, :],

import math
from contextlib import ExitStack

import concourse.mybir as mybir
from concourse.masks import make_identity

F32 = mybir.dt.float32
BF16 = mybir.dt.bfloat16
I32 = mybir.dt.int32
U32 = mybir.dt.uint32
U8 = mybir.dt.uint8
FP8X4 = mybir.dt.float8_e4m3fn_x4
ALU = mybir.AluOpType
ACT = mybir.ActivationFunctionType

P = 128
BATCH = 64
FEATURES = 16384
OUT_COLS = 512
K_PASS = 512
PASSES = FEATURES // K_PASS
WORDS_PASS = K_PASS // 2

REPLY, REVIEW = 0, 1
W_FIRST_GROUP = (PASSES, 0)

ROUND_G = 2
ROUNDS = PASSES // ROUND_G
X_CHUNK_G = 8
X_CHUNKS = PASSES // X_CHUNK_G
W_CHUNK_G = 4
W_BUFS = 8
PLANE_GROUPS = 16
MX_LAG = 6

FLOPS = 2 * 2 * P * FEATURES * OUT_COLS


def tile_positionwisedtableencoder_k_kernel(tc, review, reply, W_words, W_scales, b, out):
    nc = tc.nc
    rows = {
        REPLY: reply.rearrange("j n h -> (j n) h"),
        REVIEW: review.rearrange("j n h -> (j n) h"),
    }
    scale_words = W_scales.bitcast(I32)

    w_chunks = []
    for c in range(X_CHUNKS):
        for o in (REPLY, REVIEW):
            for first in range(c * X_CHUNK_G, (c + 1) * X_CHUNK_G, W_CHUNK_G):
                w_chunks.append((o, first))

    with ExitStack() as ctx:
        ctx.enter_context(tc.manual_schedule())
        const = ctx.enter_context(tc.tile_pool(name="const", bufs=1))
        x_pool = ctx.enter_context(tc.tile_pool(name="x", bufs=1))
        w_pool = ctx.enter_context(tc.tile_pool(name="w", bufs=W_BUFS))
        code_pool = ctx.enter_context(tc.tile_pool(name="codes", bufs=1))
        cos_pool = ctx.enter_context(tc.tile_pool(name="cospart", bufs=4))
        plane_pool = ctx.enter_context(tc.tile_pool(name="turned", bufs=2))
        group_pool = ctx.enter_context(tc.tile_pool(name="grouped", bufs=3))
        bank_pool = ctx.enter_context(tc.psum_pool(name="banks", bufs=4))
        acc_pool = ctx.enter_context(tc.psum_pool(name="acc", bufs=1))
        spread_pool = ctx.enter_context(tc.psum_pool(name="spread", bufs=1))

        x_sb = {}
        for c in range(X_CHUNKS):
            for o in (REPLY, REVIEW):
                x_tile = x_pool.tile([P, X_CHUNK_G * K_PASS], BF16, name="x%d_%d" % (o, c))
                cols = slice(c * X_CHUNK_G * K_PASS, (c + 1) * X_CHUNK_G * K_PASS)
                nc.sync.dma_start(out=x_tile[:], in_=rows[o][:, cols])
                x_sb[o, c] = x_tile

        w_planes = const.tile([P, PLANE_GROUPS, OUT_COLS], U8, name="w_planes", align_bytes=64)
        nc.vector.memset(w_planes[:].rearrange("p a n -> p (a n)").bitcast(I32), 0)
        for q in range(16):
            first_row = 32 * (q // 4) + q % 4
            nc.sync.dma_start(
                out=w_planes[first_row : first_row + 16 : 4, :, :].bitcast(I32),
                in_=scale_words[:, q, :].rearrange("(s a) n -> s a n", a=PLANE_GROUPS),
            )

        w_sb = {}

        def load_weights(w):
            o, first = w_chunks[w]
            group = W_FIRST_GROUP[o] + first
            w_tile = w_pool.tile([P, W_CHUNK_G, OUT_COLS], I32, name="w_tile", align_bytes=64)
            piece = 1
            for i in range(0, W_CHUNK_G, piece):
                nc.sync.dma_start(
                    out=w_tile[:, i : i + piece, :],
                    in_=W_words[group + i : group + i + piece].rearrange("g p n t -> p g (n t)").bitcast(I32),
                )
            w_sb[w] = w_tile

        for w in range(W_BUFS):
            load_weights(w)

        bias_row = const.tile([P, OUT_COLS], BF16, name="bias_row")
        ones = const.tile([P, P], BF16, name="ones")
        bias_sb = const.tile([P, OUT_COLS], F32, name="bias_sb")
        nc.vector.memset(bias_row[:], 0.0)
        nc.scalar.dma_start(out=bias_row[0:1, :], in_=b.unsqueeze(0))
        nc.vector.memset(ones[:], 1.0)

        def spread_bias():
            bias_ps = spread_pool.tile([P, OUT_COLS], F32, name="bias_ps", tag="spread")
            nc.tensor.matmul(out=bias_ps[:], lhsT=ones[:], rhs=bias_row[:], start=True, stop=True)
            nc.scalar.copy(out=bias_sb[:], in_=bias_ps[:])

        ident = const.tile([P, P], F32, name="ident")
        make_identity(nc, ident[:])
        pair_index = const.tile([P, 2 * PASSES], I32, name="pair_index")
        nc.gpsimd.iota(pair_index[:], pattern=[[WORDS_PASS, PASSES], [1, 2]], base=0, channel_multiplier=2)

        pair_f = const.tile([P, 2 * PASSES], F32, name="pair_f")
        angle = const.tile([P, 2 * PASSES], F32, name="angle")
        sin_tab = const.tile([P, 2 * PASSES], F32, name="sin_tab")
        neg_sin = const.tile([P, 2 * PASSES], F32, name="neg_sin")
        half_sin = const.tile([P, 2 * PASSES], F32, name="half_sin")
        half_sq = const.tile([P, 2 * PASSES], F32, name="half_sq")
        cos_tab = const.tile([P, 2 * PASSES], F32, name="cos_tab")
        nc.vector.tensor_copy(out=pair_f[:], in_=pair_index[:])
        nc.scalar.activation(out=angle[:], in_=pair_f[:], func=ACT.Exp, scale=-2.0 * math.log(10000.0) / FEATURES)
        nc.scalar.activation(out=sin_tab[:], in_=angle[:], func=ACT.Sin)
        nc.scalar.activation(out=half_sin[:], in_=angle[:], func=ACT.Sin, scale=0.5)
        nc.scalar.activation(out=half_sq[:], in_=half_sin[:], func=ACT.Square)

        perm = const.tile([P, P], F32, name="perm")
        nc.vector.tensor_copy(
            out=perm[:].rearrange("p (n j) -> p n j", n=2),
            in_=ident[:].rearrange("p (j n) -> p n j", n=2),
        )
        swap = const.tile([P, P], F32, name="swap")
        nc.vector.tensor_copy(out=swap[:, 0:BATCH], in_=ident[:, BATCH:P])
        nc.vector.tensor_copy(out=swap[:, BATCH:P], in_=ident[:, 0:BATCH])
        nc.vector.tensor_scalar(
            out=cos_tab[:], in0=half_sq[:], scalar1=-2.0, scalar2=1.0, op0=ALU.mult, op1=ALU.add
        )
        nc.vector.tensor_scalar_mul(out=neg_sin[:], in0=sin_tab[:], scalar1=-1.0)

        acc = {
            REPLY: acc_pool.tile([P, OUT_COLS], F32, name="acc_reply"),
            REVIEW: acc_pool.tile([P, OUT_COLS], F32, name="acc_review"),
        }
        banks = {}
        grouped = {}
        turned = {}
        codes = {}
        x_planes = {}

        def transpose_round(k):
            for g in range(k * ROUND_G, (k + 1) * ROUND_G):
                c, g_in_chunk = divmod(g, X_CHUNK_G)
                bank = bank_pool.tile([P, 2, 2, P], F32, name="bank")
                for o in (REPLY, REVIEW):
                    words = x_sb[o, c][:].bitcast(F32)
                    for u in range(2):
                        nc.tensor.transpose(
                            out=bank[:, o, u, :],
                            in_=words[:, g_in_chunk * WORDS_PASS + u : (g_in_chunk + 1) * WORDS_PASS : 2],
                            identity=perm[:],
                        )
                banks[g] = bank

        def rotate_round(k):
            grouped[k] = group_pool.tile([P, ROUND_G, 2, P, 4], BF16, name="grouped", align_bytes=64)
            turned[k] = plane_pool.tile([P, ROUND_G, 2, 4, BATCH], BF16, name="turned")
            for g_in_round in range(ROUND_G):
                g = k * ROUND_G + g_in_round
                bank = banks[g]
                nc.scalar.copy(
                    out=grouped[k][:, g_in_round, :, 0:BATCH, :].bitcast(F32),
                    in_=bank[:, :, :, 0:BATCH].rearrange("p o u j -> p o j u"),
                )
                position1 = bank[:].bitcast(BF16)[:, :, :, P : 2 * P]
                cos_part = cos_pool.tile([P, 2, 2, P], F32, name="cos_part")
                for u in range(2):
                    col = 2 * g + u
                    nc.scalar.activation(
                        out=cos_part[:, u, :, :],
                        in_=position1[:, :, u, :],
                        func=ACT.Copy,
                        scale=cos_tab[:, col : col + 1],
                    )
                x_pairs = position1.rearrange("p o u (j e) -> p o u j e", e=2)
                cos_pairs = cos_part[:].rearrange("p u o (j e) -> p u o j e", e=2)
                for u in range(2):
                    col = 2 * g + u
                    nc.vector.scalar_tensor_tensor(
                        out=turned[k][:, g_in_round, :, 2 * u, :],
                        in0=x_pairs[:, :, u, :, 1],
                        scalar=neg_sin[:, col : col + 1],
                        in1=cos_pairs[:, u, :, :, 0],
                        op0=ALU.mult,
                        op1=ALU.add,
                    )
                    nc.vector.scalar_tensor_tensor(
                        out=turned[k][:, g_in_round, :, 2 * u + 1, :],
                        in0=x_pairs[:, :, u, :, 0],
                        scalar=sin_tab[:, col : col + 1],
                        in1=cos_pairs[:, u, :, :, 1],
                        op0=ALU.mult,
                        op1=ALU.add,
                    )

        def regroup_round(k):
            nc.vector.tensor_copy(
                out=grouped[k][:, :, :, BATCH:P, :],
                in_=turned[k][:].rearrange("p g o t j -> p g o j t"),
            )

        def quantise_round(k):
            codes[k] = code_pool.tile([P, ROUND_G, 2, P], U32, name="codes%d" % k, align_bytes=64)
            x_planes[k] = code_pool.tile([P, ROUND_G, 2, P], U8, name="x_planes%d" % k, align_bytes=64)
            nc.vector.quantize_mx(
                out=codes[k][:].rearrange("p g o c -> p (g o c)").bitcast(FP8X4),
                scales=x_planes[k][:].rearrange("p g o c -> p (g o c)"),
                in_=grouped[k][:].rearrange("p g o c t -> p (g o c t)"),
            )

        def multiply_chunk(w):
            o, first = w_chunks[w]
            for g in range(first, first + W_CHUNK_G):
                k, g_in_round = divmod(g, ROUND_G)
                plane, block = divmod(W_FIRST_GROUP[o] + g, PLANE_GROUPS)
                nc.tensor.matmul_mx(
                    out=acc[o][:],
                    lhsT=codes[k][:, g_in_round, o, :].bitcast(FP8X4),
                    lhsT_scale=x_planes[k][:, g_in_round, o, :],
                    rhs=w_sb[w][:, g - first, :].bitcast(FP8X4),
                    rhs_scale=w_planes[4 * plane : P, block, :],
                    start=(g == 0),
                    stop=(g == PASSES - 1),
                )

        addend = const.tile([P, 2, OUT_COLS], F32, name="addend")

        def spread_reply():
            nc.vector.tensor_tensor(out=addend[:, 0, :], in0=acc[REPLY][:], in1=bias_sb[:], op=ALU.add)
            swapped = spread_pool.tile([P, OUT_COLS], F32, name="swapped", tag="spread")
            nc.tensor.matmul(out=swapped[:], lhsT=swap[:], rhs=addend[:, 0, :], start=True, stop=True)
            nc.scalar.copy(out=addend[:, 1, :], in_=swapped[:])

        for step in range(ROUNDS + MX_LAG):
            if step < ROUNDS:
                transpose_round(step)
                rotate_round(step)
            if 1 <= step <= ROUNDS:
                quantise_round(step - 1)
            if step < ROUNDS:
                regroup_round(step)
            w = step - MX_LAG
            if w == 0:
                spread_bias()
            if w >= 0:
                multiply_chunk(w)
                if w + W_BUFS < len(w_chunks):
                    load_weights(w + W_BUFS)
                if w_chunks[w] == (REPLY, PASSES - W_CHUNK_G):
                    spread_reply()

        summed = const.tile([P, 2, OUT_COLS], F32, name="summed")
        result = const.tile([P, 2, OUT_COLS], F32, name="result")
        for d in range(2):
            nc.vector.tensor_tensor(out=summed[:, d, :], in0=acc[REVIEW][:], in1=addend[:, d, :], op=ALU.add)
        for d in range(2):
            nc.vector.tensor_scalar_max(out=result[:, d, :], in0=summed[:, d, :], scalar1=0.0)
            for n in range(2):
                m = (n + d) % 2
                nc.sync.dma_start(out=out[:, n, m, :], in_=result[n * BATCH : (n + 1) * BATCH, d, :])
